import numpy as np
import ml_dtypes

BF16 = ml_dtypes.bfloat16


def bf(x):
    return np.asarray(x, np.float32).astype(BF16)


def f32(x):
    return np.asarray(x, np.float32)


def f64(x):
    return np.asarray(x).astype(np.float64)


def striped(idx):
    return np.tile(idx.reshape(-1, 16).T, (8, 1))


B, D, O, Q, C, P, S, N = 8, 128, 64, 128, 1024, 512, 3072, 1536


def sigmoid(v):
    return 1.0 / (1.0 + np.exp(-v))


def setup_inputs():
    x = f32(np.random.standard_normal((C, S)))
    adj_t = bf(np.random.uniform(-1.0, 1.0, (N, N)) * np.sqrt(3.0 / N))
    w0 = bf(np.random.uniform(-1.0, 1.0, (D, Q)) * np.sqrt(3.0 / D))
    b0 = f32(0.3 * np.random.standard_normal((Q, 1)))
    return {"x": x, "adj_t": adj_t, "w0": w0, "b0": b0, "offs": striped(np.random.permutation(S)[:N])}


def reference(x, adj_t, w0, b0, offs):
    idx = offs[:16].T.reshape(-1)
    xp = f64(x)[:, idx]
    a0 = xp @ f64(adj_t)
    lr = np.einsum("dq,rdn->rqn", f64(w0), a0.reshape(B, D, N)) + f64(b0)[None, :, :]
    h1 = (lr[:, :O, :] * sigmoid(lr[:, O:, :])).reshape(P, N)
    a1 = h1 @ f64(adj_t)
    return np.concatenate([h1, a1], axis=0)

@@ -1,0 +1,140 @@
+import concourse.mybir as mybir
+from concourse.masks import make_identity
+
+F32 = mybir.dt.float32
+BF16 = mybir.dt.bfloat16
+U16 = mybir.dt.uint16
+COPY = mybir.ActivationFunctionType.Copy
+SIGMOID = mybir.ActivationFunctionType.Sigmoid
+ADD = mybir.AluOpType.add
+MULT = mybir.AluOpType.mult
+
+P = 128
+SAMPLES = 8
+PAIRS = SAMPLES // 2
+STORE = 3072
+N = 1536
+HALF = 64
+VALUE = 0
+GATE = 1
+BLOCKS = N // P
+CHUNK = 512
+CHUNKS = N // CHUNK
+PER_BANK = CHUNK // P
+
+FLOPS = 2 * SAMPLES * P * P * N + 2 * SAMPLES * P * N * N + 2 * PAIRS * P * N * N
+
+
+def tile_stsgcm_b_kernel(tc, x, adj_t, w0, b0, offs, out):
+    nc = tc.nc
+    with (
+        tc.tile_pool(name="held", bufs=1) as held,
+        tc.tile_pool(name="work", bufs=2) as work,
+        tc.psum_pool(name="psum_mix", bufs=2) as psum_mix,
+        tc.psum_pool(name="psum_sum", bufs=4) as psum_sum,
+        tc.psum_pool(name="psum_flip", bufs=2) as psum_flip,
+    ):
+        offsets = held.tile([P, N // 16], U16, name="offsets")
+        nc.sync.dma_start(offsets[:], offs)
+
+        windows = [held.tile([P, STORE], F32, name=f"window{r}") for r in range(SAMPLES)]
+        adj = [held.tile([P, BLOCKS, CHUNK], BF16, name=f"adj{c}") for c in range(CHUNKS)]
+        adj_by_block = adj_t.rearrange("(b p) n -> p b n", p=P)
+
+        for r in range(2):
+            nc.sync.dma_start(windows[r][:], x[r * P : (r + 1) * P, :])
+        for c in range(CHUNKS):
+            nc.sync.dma_start(adj[c][:], adj_by_block[:, :, c * CHUNK : (c + 1) * CHUNK])
+        for r in range(2, SAMPLES):
+            nc.sync.dma_start(windows[r][:], x[r * P : (r + 1) * P, :])
+
+        w0_sb = held.tile([P, P], BF16, name="w0_sb")
+        nc.scalar.dma_start(w0_sb[:], w0)
+        bias = [held.tile([P, 1], F32, name=f"bias{h}") for h in (VALUE, GATE)]
+        for h in (VALUE, GATE):
+            for s in range(2):
+                nc.scalar.dma_start(
+                    bias[h][s * HALF : (s + 1) * HALF, :], b0[h * HALF : (h + 1) * HALF, :]
+                )
+
+        identity = held.tile([P, P], BF16, name="identity")
+        make_identity(nc, identity[:])
+
+        def pick_and_mix(t):
+            mixed = held.tile([P, BLOCKS, 2, P], BF16, name=f"mixed{t}")
+            for s in range(2):
+                picked = work.tile([P, N], F32, name="picked")
+                nc.scalar.activation(picked[:], windows[2 * t + s][:].indirect(offsets[:]), COPY)
+                picked_bf = work.tile([P, N], BF16, name="picked_bf")
+                nc.vector.tensor_copy(picked_bf[:], picked[:])
+                for first in range(0, BLOCKS, PER_BANK):
+                    mix_ps = psum_mix.tile([P, PER_BANK, P], F32, name="mix_ps")
+                    for i in range(PER_BANK):
+                        b = first + i
+                        nc.tensor.matmul(
+                            mix_ps[:, i, :],
+                            lhsT=picked_bf[:, b * P : (b + 1) * P],
+                            rhs=w0_sb[:],
+                            start=True,
+                            stop=True,
+                        )
+                    nc.vector.tensor_copy(
+                        mixed[:, first : first + PER_BANK, :, s * HALF : (s + 1) * HALF],
+                        mix_ps[:].rearrange("p b (h o) -> p b h o", h=2),
+                    )
+            return mixed
+
+        def sum_over_vertices(stationary, c):
+            total = psum_sum.tile([P, CHUNK], F32, name="total")
+            for b in range(BLOCKS):
+                nc.tensor.matmul(
+                    total[:],
+                    lhsT=stationary[b],
+                    rhs=adj[c][:, b, :],
+                    start=(b == 0),
+                    stop=(b == BLOCKS - 1),
+                )
+            return total
+
+        def convolve(t, mixed):
+            h1_flipped = held.tile([P, BLOCKS, P], BF16, name=f"h1_flipped{t}")
+            rows = slice(t * P, (t + 1) * P)
+            for c in range(CHUNKS):
+                columns = slice(c * CHUNK, (c + 1) * CHUNK)
+                gate_ps = sum_over_vertices([mixed[:, b, GATE, :] for b in range(BLOCKS)], c)
+                value_ps = sum_over_vertices([mixed[:, b, VALUE, :] for b in range(BLOCKS)], c)
+                gate = work.tile([P, CHUNK], F32, name="gate")
+                nc.scalar.activation(gate[:], gate_ps[:], SIGMOID, bias=bias[GATE][:])
+                h1 = work.tile([P, CHUNK], F32, name="h1")
+                nc.vector.scalar_tensor_tensor(
+                    h1[:], in0=value_ps[:], scalar=bias[VALUE][:], in1=gate[:], op0=ADD, op1=MULT
+                )
+                nc.sync.dma_start(out[rows, columns], h1[:])
+
+                h1_bf = work.tile([P, CHUNK], BF16, name="h1_bf")
+                nc.vector.tensor_copy(h1_bf[:], h1[:])
+                flip_ps = psum_flip.tile([P, PER_BANK, P], BF16, name="flip_ps")
+                for i in range(PER_BANK):
+                    nc.tensor.transpose(flip_ps[:, i, :], h1_bf[:, i * P : (i + 1) * P], identity[:])
+                nc.vector.tensor_copy(
+                    h1_flipped[:, c * PER_BANK : (c + 1) * PER_BANK, :], flip_ps[:]
+                )
+            return h1_flipped
+
+        def aggregate(t, h1_flipped):
+            rows = slice(PAIRS * P + t * P, PAIRS * P + (t + 1) * P)
+            for c in range(CHUNKS):
+                a1_ps = sum_over_vertices([h1_flipped[:, b, :] for b in range(BLOCKS)], c)
+                a1 = work.tile([P, CHUNK], F32, name="a1")
+                nc.scalar.activation(a1[:], a1_ps[:], COPY)
+                nc.sync.dma_start(out[rows, c * CHUNK : (c + 1) * CHUNK], a1[:])
+
+        mixed = [pick_and_mix(0)]
+        h1_flipped = []
+        for t in range(PAIRS):
+            if t + 1 < PAIRS:
+                mixed.append(pick_and_mix(t + 1))
+            h1_flipped.append(convolve(t, mixed[t]))
+            if t >= 1:
+                aggregate(t - 1, h1_flipped[t - 1])
+        aggregate(PAIRS - 1, h1_flipped[PAIRS - 1])

@@ -21,6 +21,7 @@ BLOCKS = N // P
 CHUNK = 512
 CHUNKS = N // CHUNK
 PER_BANK = CHUNK // P
+PIECE = PER_BANK * P
 
 FLOPS = 2 * SAMPLES * P * P * N + 2 * SAMPLES * P * N * N + 2 * PAIRS * P * N * N
 
@@ -63,17 +64,17 @@ def tile_stsgcm_b_kernel(tc, x, adj_t, w0, b0, offs, out):
         def pick_and_mix(t):
             mixed = held.tile([P, BLOCKS, 2, P], BF16, name=f"mixed{t}")
             for s in range(2):
-                picked = work.tile([P, N], F32, name="picked")
-                nc.scalar.activation(picked[:], windows[2 * t + s][:].indirect(offsets[:]), COPY)
-                picked_bf = work.tile([P, N], BF16, name="picked_bf")
-                nc.vector.tensor_copy(picked_bf[:], picked[:])
                 for first in range(0, BLOCKS, PER_BANK):
+                    piece = offsets[:, first * P // 16 : (first * P + PIECE) // 16]
+                    picked = work.tile([P, PIECE], F32, name="picked")
+                    nc.scalar.activation(picked[:], windows[2 * t + s][:].indirect(piece), COPY)
+                    picked_bf = work.tile([P, PIECE], BF16, name="picked_bf")
+                    nc.vector.tensor_copy(picked_bf[:], picked[:])
                     mix_ps = psum_mix.tile([P, PER_BANK, P], F32, name="mix_ps")
                     for i in range(PER_BANK):
-                        b = first + i
                         nc.tensor.matmul(
                             mix_ps[:, i, :],
-                            lhsT=picked_bf[:, b * P : (b + 1) * P],
+                            lhsT=picked_bf[:, i * P : (i + 1) * P],
                             rhs=w0_sb[:],
                             start=True,
                             stop=True,

@@ -22,6 +22,7 @@ CHUNK = 512
 CHUNKS = N // CHUNK
 PER_BANK = CHUNK // P
 PIECE = PER_BANK * P
+PIECES = N // PIECE
 
 FLOPS = 2 * SAMPLES * P * P * N + 2 * SAMPLES * P * N * N + 2 * PAIRS * P * N * N
 
@@ -31,6 +32,7 @@ def tile_stsgcm_b_kernel(tc, x, adj_t, w0, b0, offs, out):
     with (
         tc.tile_pool(name="held", bufs=1) as held,
         tc.tile_pool(name="work", bufs=2) as work,
+        tc.tile_pool(name="pair", bufs=2 * PIECES) as pair,
         tc.psum_pool(name="psum_mix", bufs=2) as psum_mix,
         tc.psum_pool(name="psum_sum", bufs=4) as psum_sum,
         tc.psum_pool(name="psum_flip", bufs=2) as psum_flip,
@@ -42,12 +44,17 @@ def tile_stsgcm_b_kernel(tc, x, adj_t, w0, b0, offs, out):
         adj = [held.tile([P, BLOCKS, CHUNK], BF16, name=f"adj{c}") for c in range(CHUNKS)]
         adj_by_block = adj_t.rearrange("(b p) n -> p b n", p=P)
 
-        for r in range(2):
+        def load_window(r):
             nc.sync.dma_start(windows[r][:], x[r * P : (r + 1) * P, :])
+
+        load_window(0)
+        load_window(1)
         for c in range(CHUNKS):
             nc.sync.dma_start(adj[c][:], adj_by_block[:, :, c * CHUNK : (c + 1) * CHUNK])
-        for r in range(2, SAMPLES):
-            nc.sync.dma_start(windows[r][:], x[r * P : (r + 1) * P, :])
+            if c < 2:
+                load_window(2 + c)
+        for r in range(4, SAMPLES):
+            load_window(r)
 
         w0_sb = held.tile([P, P], BF16, name="w0_sb")
         nc.scalar.dma_start(w0_sb[:], w0)
@@ -61,29 +68,37 @@ def tile_stsgcm_b_kernel(tc, x, adj_t, w0, b0, offs, out):
         identity = held.tile([P, P], BF16, name="identity")
         make_identity(nc, identity[:])
 
-        def pick_and_mix(t):
-            mixed = held.tile([P, BLOCKS, 2, P], BF16, name=f"mixed{t}")
+        scratch = held.tile([P, 1], F32, name="scratch")
+        nc.vector.memset(scratch[:], 0.0)
+        nc.scalar.activation(scratch[:], scratch[:], SIGMOID)
+
+        def look_up(t):
+            pieces = []
             for s in range(2):
-                for first in range(0, BLOCKS, PER_BANK):
-                    piece = offsets[:, first * P // 16 : (first * P + PIECE) // 16]
+                for g in range(PIECES):
+                    entries = offsets[:, g * PIECE // 16 : (g + 1) * PIECE // 16]
                     picked = work.tile([P, PIECE], F32, name="picked")
-                    nc.scalar.activation(picked[:], windows[2 * t + s][:].indirect(piece), COPY)
-                    picked_bf = work.tile([P, PIECE], BF16, name="picked_bf")
+                    nc.scalar.activation(picked[:], windows[2 * t + s][:].indirect(entries), COPY)
+                    picked_bf = pair.tile([P, PIECE], BF16, name="picked_bf")
                     nc.vector.tensor_copy(picked_bf[:], picked[:])
-                    mix_ps = psum_mix.tile([P, PER_BANK, P], F32, name="mix_ps")
-                    for i in range(PER_BANK):
-                        nc.tensor.matmul(
-                            mix_ps[:, i, :],
-                            lhsT=picked_bf[:, i * P : (i + 1) * P],
-                            rhs=w0_sb[:],
-                            start=True,
-                            stop=True,
-                        )
-                    nc.vector.tensor_copy(
-                        mixed[:, first : first + PER_BANK, :, s * HALF : (s + 1) * HALF],
-                        mix_ps[:].rearrange("p b (h o) -> p b h o", h=2),
-                    )
-            return mixed
+                    pieces.append(picked_bf)
+            return pieces
+
+        def mix(mixed_t, pieces, k):
+            s, g = divmod(k, PIECES)
+            mix_ps = psum_mix.tile([P, PER_BANK, P], F32, name="mix_ps")
+            for i in range(PER_BANK):
+                nc.tensor.matmul(
+                    mix_ps[:, i, :],
+                    lhsT=pieces[k][:, i * P : (i + 1) * P],
+                    rhs=w0_sb[:],
+                    start=True,
+                    stop=True,
+                )
+            nc.vector.tensor_copy(
+                mixed_t[:, g * PER_BANK : (g + 1) * PER_BANK, :, s * HALF : (s + 1) * HALF],
+                mix_ps[:].rearrange("p b (h o) -> p b h o", h=2),
+            )
 
         def sum_over_vertices(stationary, c):
             total = psum_sum.tile([P, CHUNK], F32, name="total")
@@ -97,45 +112,57 @@ def tile_stsgcm_b_kernel(tc, x, adj_t, w0, b0, offs, out):
                 )
             return total
 
-        def convolve(t, mixed):
-            h1_flipped = held.tile([P, BLOCKS, P], BF16, name=f"h1_flipped{t}")
-            rows = slice(t * P, (t + 1) * P)
-            for c in range(CHUNKS):
-                columns = slice(c * CHUNK, (c + 1) * CHUNK)
-                gate_ps = sum_over_vertices([mixed[:, b, GATE, :] for b in range(BLOCKS)], c)
-                value_ps = sum_over_vertices([mixed[:, b, VALUE, :] for b in range(BLOCKS)], c)
-                gate = work.tile([P, CHUNK], F32, name="gate")
-                nc.scalar.activation(gate[:], gate_ps[:], SIGMOID, bias=bias[GATE][:])
-                h1 = work.tile([P, CHUNK], F32, name="h1")
-                nc.vector.scalar_tensor_tensor(
-                    h1[:], in0=value_ps[:], scalar=bias[VALUE][:], in1=gate[:], op0=ADD, op1=MULT
-                )
-                nc.sync.dma_start(out[rows, columns], h1[:])
+        def gated_unit(t, c, gate_ps, value_ps):
+            gate = work.tile([P, CHUNK], F32, name="gate")
+            nc.scalar.activation(gate[:], gate_ps[:], SIGMOID, bias=bias[GATE][:])
+            h1 = work.tile([P, CHUNK], F32, name="h1")
+            nc.vector.scalar_tensor_tensor(
+                h1[:], in0=value_ps[:], scalar=bias[VALUE][:], in1=gate[:], op0=ADD, op1=MULT
+            )
+            nc.sync.dma_start(out[t * P : (t + 1) * P, c * CHUNK : (c + 1) * CHUNK], h1[:])
+            h1_bf = work.tile([P, CHUNK], BF16, name="h1_bf")
+            nc.vector.tensor_copy(h1_bf[:], h1[:])
+            return h1_bf
 
-                h1_bf = work.tile([P, CHUNK], BF16, name="h1_bf")
-                nc.vector.tensor_copy(h1_bf[:], h1[:])
-                flip_ps = psum_flip.tile([P, PER_BANK, P], BF16, name="flip_ps")
-                for i in range(PER_BANK):
-                    nc.tensor.transpose(flip_ps[:, i, :], h1_bf[:, i * P : (i + 1) * P], identity[:])
-                nc.vector.tensor_copy(
-                    h1_flipped[:, c * PER_BANK : (c + 1) * PER_BANK, :], flip_ps[:]
-                )
-            return h1_flipped
+        def flip(t, c, h1_bf):
+            flip_ps = psum_flip.tile([P, PER_BANK, P], BF16, name="flip_ps")
+            for i in range(PER_BANK):
+                nc.tensor.transpose(flip_ps[:, i, :], h1_bf[:, i * P : (i + 1) * P], identity[:])
+            nc.vector.tensor_copy(h1_flipped[t][:, c * PER_BANK : (c + 1) * PER_BANK, :], flip_ps[:])
 
-        def aggregate(t, h1_flipped):
-            rows = slice(PAIRS * P + t * P, PAIRS * P + (t + 1) * P)
-            for c in range(CHUNKS):
-                a1_ps = sum_over_vertices([h1_flipped[:, b, :] for b in range(BLOCKS)], c)
-                a1 = work.tile([P, CHUNK], F32, name="a1")
-                nc.scalar.activation(a1[:], a1_ps[:], COPY)
-                nc.sync.dma_start(out[rows, c * CHUNK : (c + 1) * CHUNK], a1[:])
+        def aggregate(t, c):
+            a1_ps = sum_over_vertices([h1_flipped[t][:, b, :] for b in range(BLOCKS)], c)
+            a1 = work.tile([P, CHUNK], F32, name="a1")
+            nc.scalar.activation(a1[:], a1_ps[:], COPY)
+            rows = slice((PAIRS + t) * P, (PAIRS + t + 1) * P)
+            nc.sync.dma_start(out[rows, c * CHUNK : (c + 1) * CHUNK], a1[:])
 
-        mixed = [pick_and_mix(0)]
-        h1_flipped = []
+        mixed = [held.tile([P, BLOCKS, 2, P], BF16, name=f"mixed{t}") for t in range(PAIRS)]
+        h1_flipped = [held.tile([P, BLOCKS, P], BF16, name=f"h1_flipped{t}") for t in range(PAIRS)]
+
+        pieces = look_up(0)
+        for k in range(2 * PIECES):
+            mix(mixed[0], pieces, k)
         for t in range(PAIRS):
-            if t + 1 < PAIRS:
-                mixed.append(pick_and_mix(t + 1))
-            h1_flipped.append(convolve(t, mixed[t]))
-            if t >= 1:
-                aggregate(t - 1, h1_flipped[t - 1])
-        aggregate(PAIRS - 1, h1_flipped[PAIRS - 1])
+            more = t + 1 < PAIRS
+            if more:
+                pieces = look_up(t + 1)
+            h1_bf = []
+            for c in range(CHUNKS):
+                gate_ps = sum_over_vertices([mixed[t][:, b, GATE, :] for b in range(BLOCKS)], c)
+                if more:
+                    mix(mixed[t + 1], pieces, 2 * c)
+                value_ps = sum_over_vertices([mixed[t][:, b, VALUE, :] for b in range(BLOCKS)], c)
+                if more:
+                    mix(mixed[t + 1], pieces, 2 * c + 1)
+                h1_bf.append(gated_unit(t, c, gate_ps, value_ps))
+                if c > 0:
+                    flip(t, c - 1, h1_bf[c - 1])
+            if t > 0:
+                aggregate(t - 1, 0)
+            flip(t, CHUNKS - 1, h1_bf[CHUNKS - 1])
+            if t > 0:
+                aggregate(t - 1, 1)
+                aggregate(t - 1, 2)
+        for c in range(CHUNKS):
+            aggregate(PAIRS - 1, c)

@@ -23,6 +23,7 @@ CHUNKS = N // CHUNK
 PER_BANK = CHUNK // P
 PIECE = PER_BANK * P
 PIECES = N // PIECE
+SHORT = PIECE // 2
 
 FLOPS = 2 * SAMPLES * P * P * N + 2 * SAMPLES * P * N * N + 2 * PAIRS * P * N * N
 
@@ -32,27 +33,27 @@ def tile_stsgcm_b_kernel(tc, x, adj_t, w0, b0, offs, out):
     with (
         tc.tile_pool(name="held", bufs=1) as held,
         tc.tile_pool(name="work", bufs=2) as work,
-        tc.tile_pool(name="pair", bufs=2 * PIECES) as pair,
-        tc.psum_pool(name="psum_mix", bufs=2) as psum_mix,
-        tc.psum_pool(name="psum_sum", bufs=4) as psum_sum,
-        tc.psum_pool(name="psum_flip", bufs=2) as psum_flip,
+        tc.tile_pool(name="pair", bufs=2 * N // SHORT) as pair,
+        tc.tile_pool(name="rounded", bufs=CHUNKS + 1) as rounded,
+        tc.tile_pool(name="stored", bufs=4) as stored,
+        tc.psum_pool(name="psum_small", bufs=2) as psum_small,
+        tc.psum_pool(name="psum_sum", bufs=2 * CHUNKS) as psum_sum,
     ):
         offsets = held.tile([P, N // 16], U16, name="offsets")
         nc.sync.dma_start(offsets[:], offs)
 
         windows = [held.tile([P, STORE], F32, name=f"window{r}") for r in range(SAMPLES)]
-        adj = [held.tile([P, BLOCKS, CHUNK], BF16, name=f"adj{c}") for c in range(CHUNKS)]
-        adj_by_block = adj_t.rearrange("(b p) n -> p b n", p=P)
+        adj = [held.tile([P, N], BF16, name=f"adj{b}") for b in range(BLOCKS)]
 
         def load_window(r):
             nc.sync.dma_start(windows[r][:], x[r * P : (r + 1) * P, :])
 
         load_window(0)
         load_window(1)
-        for c in range(CHUNKS):
-            nc.sync.dma_start(adj[c][:], adj_by_block[:, :, c * CHUNK : (c + 1) * CHUNK])
-            if c < 2:
-                load_window(2 + c)
+        for b in range(BLOCKS):
+            nc.sync.dma_start(adj[b][:], adj_t[b * P : (b + 1) * P, :])
+            if b == 3 or b == 7:
+                load_window(2 + b // 4)
         for r in range(4, SAMPLES):
             load_window(r)
 
@@ -72,97 +73,128 @@ def tile_stsgcm_b_kernel(tc, x, adj_t, w0, b0, offs, out):
         nc.vector.memset(scratch[:], 0.0)
         nc.scalar.activation(scratch[:], scratch[:], SIGMOID)
 
-        def look_up(t):
-            pieces = []
-            for s in range(2):
-                for g in range(PIECES):
-                    entries = offsets[:, g * PIECE // 16 : (g + 1) * PIECE // 16]
-                    picked = work.tile([P, PIECE], F32, name="picked")
-                    nc.scalar.activation(picked[:], windows[2 * t + s][:].indirect(entries), COPY)
-                    picked_bf = pair.tile([P, PIECE], BF16, name="picked_bf")
-                    nc.vector.tensor_copy(picked_bf[:], picked[:])
-                    pieces.append(picked_bf)
-            return pieces
+        def look_up(r, first, width):
+            entries = offsets[:, first // 16 : (first + width) // 16]
+            picked = work.tile([P, width], F32, name="picked")
+            nc.scalar.activation(picked[:], windows[r][:].indirect(entries), COPY)
+            picked_bf = pair.tile([P, width], BF16, name="picked_bf")
+            nc.vector.tensor_copy(picked_bf[:], picked[:])
+            return picked_bf
 
-        def mix(mixed_t, pieces, k):
-            s, g = divmod(k, PIECES)
-            mix_ps = psum_mix.tile([P, PER_BANK, P], F32, name="mix_ps")
-            for i in range(PER_BANK):
+        def look_up_pair(t):
+            return [
+                (r, g * PIECE, look_up(r, g * PIECE, PIECE))
+                for r in (2 * t, 2 * t + 1)
+                for g in range(PIECES)
+            ]
+
+        def mix(r, first, picked_bf):
+            t, s = divmod(r, 2)
+            blocks = picked_bf.shape[1] // P
+            mix_ps = psum_small.tile([P, blocks, P], F32, name="mix_ps", tag="small")
+            for i in range(blocks):
                 nc.tensor.matmul(
                     mix_ps[:, i, :],
-                    lhsT=pieces[k][:, i * P : (i + 1) * P],
+                    lhsT=picked_bf[:, i * P : (i + 1) * P],
                     rhs=w0_sb[:],
                     start=True,
                     stop=True,
                 )
             nc.vector.tensor_copy(
-                mixed_t[:, g * PER_BANK : (g + 1) * PER_BANK, :, s * HALF : (s + 1) * HALF],
+                mixed[t][:, first // P : first // P + blocks, :, s * HALF : (s + 1) * HALF],
                 mix_ps[:].rearrange("p b (h o) -> p b h o", h=2),
             )
 
-        def sum_over_vertices(stationary, c):
-            total = psum_sum.tile([P, CHUNK], F32, name="total")
+        def add_block(total, stationary, b, first):
+            nc.tensor.matmul(
+                total[:],
+                lhsT=stationary,
+                rhs=adj[b][:, first : first + total.shape[1]],
+                start=(b == 0),
+                stop=(b == BLOCKS - 1),
+            )
+
+        def sum_over_vertices(stationary, first, width):
+            total = psum_sum.tile([P, width], F32, name="total")
             for b in range(BLOCKS):
-                nc.tensor.matmul(
-                    total[:],
-                    lhsT=stationary[b],
-                    rhs=adj[c][:, b, :],
-                    start=(b == 0),
-                    stop=(b == BLOCKS - 1),
-                )
+                add_block(total, stationary[b], b, first)
             return total
 
         def gated_unit(t, c, gate_ps, value_ps):
             gate = work.tile([P, CHUNK], F32, name="gate")
             nc.scalar.activation(gate[:], gate_ps[:], SIGMOID, bias=bias[GATE][:])
-            h1 = work.tile([P, CHUNK], F32, name="h1")
+            h1 = stored.tile([P, CHUNK], F32, name="h1")
             nc.vector.scalar_tensor_tensor(
                 h1[:], in0=value_ps[:], scalar=bias[VALUE][:], in1=gate[:], op0=ADD, op1=MULT
             )
             nc.sync.dma_start(out[t * P : (t + 1) * P, c * CHUNK : (c + 1) * CHUNK], h1[:])
-            h1_bf = work.tile([P, CHUNK], BF16, name="h1_bf")
+            h1_bf = rounded.tile([P, CHUNK], BF16, name="h1_bf")
             nc.vector.tensor_copy(h1_bf[:], h1[:])
             return h1_bf
 
         def flip(t, c, h1_bf):
-            flip_ps = psum_flip.tile([P, PER_BANK, P], BF16, name="flip_ps")
+            flip_ps = psum_small.tile([P, PER_BANK, P], BF16, name="flip_ps", tag="small")
             for i in range(PER_BANK):
                 nc.tensor.transpose(flip_ps[:, i, :], h1_bf[:, i * P : (i + 1) * P], identity[:])
             nc.vector.tensor_copy(h1_flipped[t][:, c * PER_BANK : (c + 1) * PER_BANK, :], flip_ps[:])
 
-        def aggregate(t, c):
-            a1_ps = sum_over_vertices([h1_flipped[t][:, b, :] for b in range(BLOCKS)], c)
-            a1 = work.tile([P, CHUNK], F32, name="a1")
-            nc.scalar.activation(a1[:], a1_ps[:], COPY)
-            rows = slice((PAIRS + t) * P, (PAIRS + t + 1) * P)
-            nc.sync.dma_start(out[rows, c * CHUNK : (c + 1) * CHUNK], a1[:])
+        def aggregate(t, first, width):
+            a1_ps = sum_over_vertices([h1_flipped[t][:, b, :] for b in range(BLOCKS)], first, width)
+            a1 = stored.tile([P, width], F32, name="a1")
+            nc.vector.tensor_copy(a1[:], a1_ps[:])
+            nc.sync.dma_start(out[(PAIRS + t) * P : (PAIRS + t + 1) * P, first : first + width], a1[:])
 
         mixed = [held.tile([P, BLOCKS, 2, P], BF16, name=f"mixed{t}") for t in range(PAIRS)]
         h1_flipped = [held.tile([P, BLOCKS, P], BF16, name=f"h1_flipped{t}") for t in range(PAIRS)]
 
-        pieces = look_up(0)
-        for k in range(2 * PIECES):
-            mix(mixed[0], pieces, k)
-        for t in range(PAIRS):
+
+        short_pieces = [
+            (r, first, look_up(r, first, SHORT)) for first in range(0, N, SHORT) for r in range(2)
+        ]
+        totals = [
+            [psum_sum.tile([P, CHUNK], F32, name="total") for c in range(CHUNKS)]
+            for h in (VALUE, GATE)
+        ]
+        first_of_next = BLOCKS - 2 * PIECES
+        for r in range(2):
+            mix(*short_pieces[r])
+        for b in range(BLOCKS):
+            if b % (SHORT // P) == 0 and b + SHORT // P < BLOCKS:
+                for r in range(2):
+                    mix(*short_pieces[(b * P // SHORT + 1) * 2 + r])
+            for h in (GATE, VALUE):
+                for c in range(CHUNKS):
+                    add_block(totals[h][c], mixed[0][:, b, h, :], b, c * CHUNK)
+            if b == first_of_next - 2:
+                pieces = look_up_pair(1)
+            if b >= first_of_next:
+                mix(*pieces[b - first_of_next])
+        h1_bf = [gated_unit(0, c, totals[GATE][c], totals[VALUE][c]) for c in range(CHUNKS)]
+
+        for t in range(1, PAIRS):
             more = t + 1 < PAIRS
             if more:
-                pieces = look_up(t + 1)
+                pieces = look_up_pair(t + 1)
+            earlier_bf = h1_bf
             h1_bf = []
             for c in range(CHUNKS):
-                gate_ps = sum_over_vertices([mixed[t][:, b, GATE, :] for b in range(BLOCKS)], c)
+                gate_ps = sum_over_vertices(
+                    [mixed[t][:, b, GATE, :] for b in range(BLOCKS)], c * CHUNK, CHUNK
+                )
                 if more:
-                    mix(mixed[t + 1], pieces, 2 * c)
-                value_ps = sum_over_vertices([mixed[t][:, b, VALUE, :] for b in range(BLOCKS)], c)
+                    mix(*pieces[2 * c])
+                value_ps = sum_over_vertices(
+                    [mixed[t][:, b, VALUE, :] for b in range(BLOCKS)], c * CHUNK, CHUNK
+                )
                 if more:
-                    mix(mixed[t + 1], pieces, 2 * c + 1)
+                    mix(*pieces[2 * c + 1])
+                flip(t - 1, c, earlier_bf[c])
                 h1_bf.append(gated_unit(t, c, gate_ps, value_ps))
-                if c > 0:
-                    flip(t, c - 1, h1_bf[c - 1])
-            if t > 0:
-                aggregate(t - 1, 0)
-            flip(t, CHUNKS - 1, h1_bf[CHUNKS - 1])
-            if t > 0:
-                aggregate(t - 1, 1)
-                aggregate(t - 1, 2)
-        for c in range(CHUNKS):
-            aggregate(PAIRS - 1, c)
+            for c in range(CHUNKS):
+                aggregate(t - 1, c * CHUNK, CHUNK)
+                if not more:
+                    flip(t, c, h1_bf[c])
+        for c in range(CHUNKS - 1):
+            aggregate(PAIRS - 1, c * CHUNK, CHUNK)
+        for first in range(N - CHUNK, N, P):
+            aggregate(PAIRS - 1, first, P)

@@ -114,10 +114,19 @@ def tile_stsgcm_b_kernel(tc, x, adj_t, w0, b0, offs, out):
                 stop=(b == BLOCKS - 1),
             )
 
-        def sum_over_vertices(stationary, first, width):
+        def sum_over_vertices(stationary, first, width, to_flip=None):
             total = psum_sum.tile([P, width], F32, name="total")
+            if to_flip is not None:
+                t, c, h1_bf = to_flip
+                flip_ps = psum_small.tile([P, PER_BANK, P], BF16, name="flip_ps", tag="small")
             for b in range(BLOCKS):
                 add_block(total, stationary[b], b, first)
+                if to_flip is not None and b < PER_BANK:
+                    nc.tensor.transpose(flip_ps[:, b, :], h1_bf[:, b * P : (b + 1) * P], identity[:])
+            if to_flip is not None:
+                nc.vector.tensor_copy(
+                    h1_flipped[t][:, c * PER_BANK : (c + 1) * PER_BANK, :], flip_ps[:]
+                )
             return total
 
         def gated_unit(t, c, gate_ps, value_ps):
@@ -132,14 +141,10 @@ def tile_stsgcm_b_kernel(tc, x, adj_t, w0, b0, offs, out):
             nc.vector.tensor_copy(h1_bf[:], h1[:])
             return h1_bf
 
-        def flip(t, c, h1_bf):
-            flip_ps = psum_small.tile([P, PER_BANK, P], BF16, name="flip_ps", tag="small")
-            for i in range(PER_BANK):
-                nc.tensor.transpose(flip_ps[:, i, :], h1_bf[:, i * P : (i + 1) * P], identity[:])
-            nc.vector.tensor_copy(h1_flipped[t][:, c * PER_BANK : (c + 1) * PER_BANK, :], flip_ps[:])
-
-        def aggregate(t, first, width):
-            a1_ps = sum_over_vertices([h1_flipped[t][:, b, :] for b in range(BLOCKS)], first, width)
+        def aggregate(t, first, width, to_flip=None):
+            a1_ps = sum_over_vertices(
+                [h1_flipped[t][:, b, :] for b in range(BLOCKS)], first, width, to_flip
+            )
             a1 = stored.tile([P, width], F32, name="a1")
             nc.vector.tensor_copy(a1[:], a1_ps[:])
             nc.sync.dma_start(out[(PAIRS + t) * P : (PAIRS + t + 1) * P, first : first + width], a1[:])
@@ -184,16 +189,16 @@ def tile_stsgcm_b_kernel(tc, x, adj_t, w0, b0, offs, out):
                 if more:
                     mix(*pieces[2 * c])
                 value_ps = sum_over_vertices(
-                    [mixed[t][:, b, VALUE, :] for b in range(BLOCKS)], c * CHUNK, CHUNK
+                    [mixed[t][:, b, VALUE, :] for b in range(BLOCKS)],
+                    c * CHUNK,
+                    CHUNK,
+                    to_flip=(t - 1, c, earlier_bf[c]),
                 )
                 if more:
                     mix(*pieces[2 * c + 1])
-                flip(t - 1, c, earlier_bf[c])
                 h1_bf.append(gated_unit(t, c, gate_ps, value_ps))
             for c in range(CHUNKS):
-                aggregate(t - 1, c * CHUNK, CHUNK)
-                if not more:
-                    flip(t, c, h1_bf[c])
+                aggregate(t - 1, c * CHUNK, CHUNK, to_flip=None if more else (t, c, h1_bf[c]))
         for c in range(CHUNKS - 1):
             aggregate(PAIRS - 1, c * CHUNK, CHUNK)
         for first in range(N - CHUNK, N, P):

@@ -24,6 +24,8 @@ PER_BANK = CHUNK // P
 PIECE = PER_BANK * P
 PIECES = N // PIECE
 SHORT = PIECE // 2
+SHORTS = N // SHORT
+AHEAD = 4
 
 FLOPS = 2 * SAMPLES * P * P * N + 2 * SAMPLES * P * N * N + 2 * PAIRS * P * N * N
 
@@ -33,9 +35,9 @@ def tile_stsgcm_b_kernel(tc, x, adj_t, w0, b0, offs, out):
     with (
         tc.tile_pool(name="held", bufs=1) as held,
         tc.tile_pool(name="work", bufs=2) as work,
-        tc.tile_pool(name="pair", bufs=2 * N // SHORT) as pair,
+        tc.tile_pool(name="pair", bufs=2 * SHORTS + 1) as pair,
         tc.tile_pool(name="rounded", bufs=CHUNKS + 1) as rounded,
-        tc.tile_pool(name="stored", bufs=4) as stored,
+        tc.tile_pool(name="stored", bufs=2) as stored,
         tc.psum_pool(name="psum_small", bufs=2) as psum_small,
         tc.psum_pool(name="psum_sum", bufs=2 * CHUNKS) as psum_sum,
     ):
@@ -54,17 +56,17 @@ def tile_stsgcm_b_kernel(tc, x, adj_t, w0, b0, offs, out):
             nc.sync.dma_start(adj[b][:], adj_t[b * P : (b + 1) * P, :])
             if b == 3 or b == 7:
                 load_window(2 + b // 4)
+        bias = [held.tile([P, 1], F32, name=f"bias{h}") for h in (VALUE, GATE)]
+        for h in (VALUE, GATE):
+            for s in range(2):
+                nc.sync.dma_start(
+                    bias[h][s * HALF : (s + 1) * HALF, :], b0[h * HALF : (h + 1) * HALF, :]
+                )
         for r in range(4, SAMPLES):
             load_window(r)
 
         w0_sb = held.tile([P, P], BF16, name="w0_sb")
         nc.scalar.dma_start(w0_sb[:], w0)
-        bias = [held.tile([P, 1], F32, name=f"bias{h}") for h in (VALUE, GATE)]
-        for h in (VALUE, GATE):
-            for s in range(2):
-                nc.scalar.dma_start(
-                    bias[h][s * HALF : (s + 1) * HALF, :], b0[h * HALF : (h + 1) * HALF, :]
-                )
 
         identity = held.tile([P, P], BF16, name="identity")
         make_identity(nc, identity[:])
@@ -153,23 +155,26 @@ def tile_stsgcm_b_kernel(tc, x, adj_t, w0, b0, offs, out):
         h1_flipped = [held.tile([P, BLOCKS, P], BF16, name=f"h1_flipped{t}") for t in range(PAIRS)]
 
 
-        short_pieces = [
-            (r, first, look_up(r, first, SHORT)) for first in range(0, N, SHORT) for r in range(2)
-        ]
+        short_order = (
+            [(0, k * SHORT, SHORT) for k in range(AHEAD)]
+            + [(1, 0, SHORT // 2), (1, SHORT // 2, SHORT // 2)]
+            + [(1, k * SHORT, SHORT) for k in range(1, AHEAD)]
+            + [(r, k * SHORT, SHORT) for k in range(AHEAD, SHORTS) for r in range(2)]
+        )
+        short_pieces = [(r, first, look_up(r, first, width)) for r, first, width in short_order]
         totals = [
             [psum_sum.tile([P, CHUNK], F32, name="total") for c in range(CHUNKS)]
             for h in (VALUE, GATE)
         ]
         first_of_next = BLOCKS - 2 * PIECES
-        for r in range(2):
-            mix(*short_pieces[r])
+        for piece in short_pieces[: AHEAD + 2]:
+            mix(*piece)
         for b in range(BLOCKS):
-            if b % (SHORT // P) == 0 and b + SHORT // P < BLOCKS:
-                for r in range(2):
-                    mix(*short_pieces[(b * P // SHORT + 1) * 2 + r])
             for h in (GATE, VALUE):
                 for c in range(CHUNKS):
                     add_block(totals[h][c], mixed[0][:, b, h, :], b, c * CHUNK)
+            if AHEAD + 2 + b < len(short_pieces):
+                mix(*short_pieces[AHEAD + 2 + b])
             if b == first_of_next - 2:
                 pieces = look_up_pair(1)
             if b >= first_of_next:
@@ -201,5 +206,5 @@ def tile_stsgcm_b_kernel(tc, x, adj_t, w0, b0, offs, out):
                 aggregate(t - 1, c * CHUNK, CHUNK, to_flip=None if more else (t, c, h1_bf[c]))
         for c in range(CHUNKS - 1):
             aggregate(PAIRS - 1, c * CHUNK, CHUNK)
-        for first in range(N - CHUNK, N, P):
-            aggregate(PAIRS - 1, first, P)
+        aggregate(PAIRS - 1, N - CHUNK, CHUNK - P)
+        aggregate(PAIRS - 1, N - P, P)

@@ -23,9 +23,10 @@ CHUNKS = N // CHUNK
 PER_BANK = CHUNK // P
 PIECE = PER_BANK * P
 PIECES = N // PIECE
-SHORT = PIECE // 2
+SHORT = 2 * P
 SHORTS = N // SHORT
-AHEAD = 4
+LEAD = BLOCKS // 2
+LAG = 2
 
 FLOPS = 2 * SAMPLES * P * P * N + 2 * SAMPLES * P * N * N + 2 * PAIRS * P * N * N
 
@@ -35,8 +36,9 @@ def tile_stsgcm_b_kernel(tc, x, adj_t, w0, b0, offs, out):
     with (
         tc.tile_pool(name="held", bufs=1) as held,
         tc.tile_pool(name="work", bufs=2) as work,
-        tc.tile_pool(name="pair", bufs=2 * SHORTS + 1) as pair,
-        tc.tile_pool(name="rounded", bufs=CHUNKS + 1) as rounded,
+        tc.tile_pool(name="pair", bufs=2 * (SHORTS + 1)) as pair,
+        tc.tile_pool(name="swap", bufs=CHUNKS) as swap,
+        tc.tile_pool(name="rounded", bufs=(LAG + 1) * CHUNKS) as rounded,
         tc.tile_pool(name="stored", bufs=2) as stored,
         tc.psum_pool(name="psum_small", bufs=2) as psum_small,
         tc.psum_pool(name="psum_sum", bufs=2 * CHUNKS) as psum_sum,
@@ -51,11 +53,10 @@ def tile_stsgcm_b_kernel(tc, x, adj_t, w0, b0, offs, out):
             nc.sync.dma_start(windows[r][:], x[r * P : (r + 1) * P, :])
 
         load_window(0)
-        load_window(1)
         for b in range(BLOCKS):
             nc.sync.dma_start(adj[b][:], adj_t[b * P : (b + 1) * P, :])
-            if b == 3 or b == 7:
-                load_window(2 + b // 4)
+            if b in (3, 5, 7):
+                load_window((b - 1) // 2)
         bias = [held.tile([P, 1], F32, name=f"bias{h}") for h in (VALUE, GATE)]
         for h in (VALUE, GATE):
             for s in range(2):
@@ -67,6 +68,10 @@ def tile_stsgcm_b_kernel(tc, x, adj_t, w0, b0, offs, out):
 
         w0_sb = held.tile([P, P], BF16, name="w0_sb")
         nc.scalar.dma_start(w0_sb[:], w0)
+
+        w0_swapped = held.tile([P, P], BF16, name="w0_swapped")
+        nc.vector.tensor_copy(w0_swapped[:, :HALF], w0_sb[:, HALF:])
+        nc.vector.tensor_copy(w0_swapped[:, HALF:], w0_sb[:, :HALF])
 
         identity = held.tile([P, P], BF16, name="identity")
         make_identity(nc, identity[:])
@@ -98,14 +103,17 @@ def tile_stsgcm_b_kernel(tc, x, adj_t, w0, b0, offs, out):
                 nc.tensor.matmul(
                     mix_ps[:, i, :],
                     lhsT=picked_bf[:, i * P : (i + 1) * P],
-                    rhs=w0_sb[:],
+                    rhs=w0_swapped[:] if r == 1 else w0_sb[:],
                     start=True,
                     stop=True,
                 )
-            nc.vector.tensor_copy(
-                mixed[t][:, first // P : first // P + blocks, :, s * HALF : (s + 1) * HALF],
-                mix_ps[:].rearrange("p b (h o) -> p b h o", h=2),
-            )
+            if t == 0:
+                nc.vector.tensor_copy(alone[:, first // P : first // P + blocks, s, :], mix_ps[:])
+            else:
+                nc.vector.tensor_copy(
+                    mixed[t][:, first // P : first // P + blocks, :, s * HALF : (s + 1) * HALF],
+                    mix_ps[:].rearrange("p b (h o) -> p b h o", h=2),
+                )
 
         def add_block(total, stationary, b, first):
             nc.tensor.matmul(
@@ -151,42 +159,79 @@ def tile_stsgcm_b_kernel(tc, x, adj_t, w0, b0, offs, out):
             nc.vector.tensor_copy(a1[:], a1_ps[:])
             nc.sync.dma_start(out[(PAIRS + t) * P : (PAIRS + t + 1) * P, first : first + width], a1[:])
 
-        mixed = [held.tile([P, BLOCKS, 2, P], BF16, name=f"mixed{t}") for t in range(PAIRS)]
+        mixed = [None] + [held.tile([P, BLOCKS, 2, P], BF16, name=f"mixed{t}") for t in range(1, PAIRS)]
+        alone = held.tile([P, BLOCKS, 2, P], BF16, name="alone")
         h1_flipped = [held.tile([P, BLOCKS, P], BF16, name=f"h1_flipped{t}") for t in range(PAIRS)]
 
 
-        short_order = (
-            [(0, k * SHORT, SHORT) for k in range(AHEAD)]
-            + [(1, 0, SHORT // 2), (1, SHORT // 2, SHORT // 2)]
-            + [(1, k * SHORT, SHORT) for k in range(1, AHEAD)]
-            + [(r, k * SHORT, SHORT) for k in range(AHEAD, SHORTS) for r in range(2)]
+        units = (
+            [(0, b) for b in range(LEAD)]
+            + [(1, b) for b in range(LEAD)]
+            + [(s, b) for b in range(LEAD, BLOCKS) for s in range(2)]
         )
-        short_pieces = [(r, first, look_up(r, first, width)) for r, first, width in short_order]
-        totals = [
-            [psum_sum.tile([P, CHUNK], F32, name="total") for c in range(CHUNKS)]
-            for h in (VALUE, GATE)
+        firsts = [0, P] + [k * SHORT for k in range(1, SHORTS)]
+        widths = [P, P] + [SHORT] * (SHORTS - 1)
+        shorts = {
+            (s, first // P): (s, first, look_up(s, first, width))
+            for s in range(2)
+            for first, width in zip(firsts, widths)
+        }
+
+        def mix_short(n):
+            if n < len(units) and units[n] in shorts:
+                mix(*shorts[units[n]])
+
+        both = [
+            [psum_sum.tile([P, CHUNK], F32, name="total") for c in range(CHUNKS)] for s in range(2)
         ]
-        first_of_next = BLOCKS - 2 * PIECES
-        for piece in short_pieces[: AHEAD + 2]:
-            mix(*piece)
-        for b in range(BLOCKS):
-            for h in (GATE, VALUE):
-                for c in range(CHUNKS):
-                    add_block(totals[h][c], mixed[0][:, b, h, :], b, c * CHUNK)
-            if AHEAD + 2 + b < len(short_pieces):
-                mix(*short_pieces[AHEAD + 2 + b])
-            if b == first_of_next - 2:
+        first_of_next = len(units) - 4 * PIECES
+        mix_short(0)
+        mix_short(1)
+        for n, (s, b) in enumerate(units):
+            mix_short(n + 2)
+            for c in range(CHUNKS):
+                add_block(both[s][c], alone[:, b, s, :], b, c * CHUNK)
+            if n == first_of_next - 4:
                 pieces = look_up_pair(1)
-            if b >= first_of_next:
-                mix(*pieces[b - first_of_next])
-        h1_bf = [gated_unit(0, c, totals[GATE][c], totals[VALUE][c]) for c in range(CHUNKS)]
+            if n >= first_of_next and n % 2 == 1:
+                mix(*pieces[(n - first_of_next) // 2])
+
+        value_rows = [slice(s * HALF, (s + 1) * HALF) for s in range(2)]
+        gate_rows = [slice((1 - s) * HALF, (2 - s) * HALF) for s in range(2)]
+        bias_alone = [held.tile([P, 1], F32, name=f"bias_alone{s}") for s in range(2)]
+        for s in range(2):
+            nc.vector.tensor_copy(bias_alone[s][value_rows[s], :], bias[VALUE][value_rows[s], :])
+            nc.vector.tensor_copy(bias_alone[s][gate_rows[s], :], bias[GATE][gate_rows[s], :])
+        lr = [[swap.tile([P, CHUNK], F32, name=f"lr{s}") for c in range(CHUNKS)] for s in range(2)]
+        for s in range(2):
+            for c in range(CHUNKS):
+                nc.vector.tensor_scalar_add(lr[s][c][:], both[s][c][:], bias_alone[s][:])
+
+        pieces = look_up_pair(2)
+
+        h1_bf = {0: []}
+        for c in range(CHUNKS):
+            moved = swap.tile([P, CHUNK], F32, name="moved")
+            h1 = swap.tile([P, CHUNK], F32, name="h1_late")
+            for s in range(2):
+                nc.scalar.activation(lr[s][c][gate_rows[s], :], lr[s][c][gate_rows[s], :], SIGMOID)
+                nc.sync.dma_start(moved[value_rows[s], :], lr[s][c][gate_rows[s], :])
+                nc.gpsimd.tensor_tensor(
+                    h1[value_rows[s], :], lr[s][c][value_rows[s], :], moved[value_rows[s], :], MULT
+                )
+            nc.sync.dma_start(out[:P, c * CHUNK : (c + 1) * CHUNK], h1[:])
+            rounded_h1 = rounded.tile([P, CHUNK], BF16, name="h1_bf")
+            nc.gpsimd.tensor_copy(rounded_h1[:], h1[:])
+            h1_bf[0].append(rounded_h1)
+
+        def aggregate_pair(u):
+            late = PAIRS - LAG <= u + 1 < PAIRS
+            for c in range(CHUNKS if u + 1 < PAIRS else CHUNKS - 1):
+                aggregate(u, c * CHUNK, CHUNK, to_flip=(u + 1, c, h1_bf[u + 1][c]) if late else None)
 
         for t in range(1, PAIRS):
             more = t + 1 < PAIRS
-            if more:
-                pieces = look_up_pair(t + 1)
-            earlier_bf = h1_bf
-            h1_bf = []
+            h1_bf[t] = []
             for c in range(CHUNKS):
                 gate_ps = sum_over_vertices(
                     [mixed[t][:, b, GATE, :] for b in range(BLOCKS)], c * CHUNK, CHUNK
@@ -197,14 +242,16 @@ def tile_stsgcm_b_kernel(tc, x, adj_t, w0, b0, offs, out):
                     [mixed[t][:, b, VALUE, :] for b in range(BLOCKS)],
                     c * CHUNK,
                     CHUNK,
-                    to_flip=(t - 1, c, earlier_bf[c]),
+                    to_flip=(t - LAG, c, h1_bf[t - LAG][c]) if t >= LAG else None,
                 )
                 if more:
                     mix(*pieces[2 * c + 1])
-                h1_bf.append(gated_unit(t, c, gate_ps, value_ps))
-            for c in range(CHUNKS):
-                aggregate(t - 1, c * CHUNK, CHUNK, to_flip=None if more else (t, c, h1_bf[c]))
-        for c in range(CHUNKS - 1):
-            aggregate(PAIRS - 1, c * CHUNK, CHUNK)
+                h1_bf[t].append(gated_unit(t, c, gate_ps, value_ps))
+            if t + 2 < PAIRS:
+                pieces = look_up_pair(t + 2)
+            if t >= LAG:
+                aggregate_pair(t - LAG)
+        for u in range(PAIRS - LAG, PAIRS):
+            aggregate_pair(u)
         aggregate(PAIRS - 1, N - CHUNK, CHUNK - P)
         aggregate(PAIRS - 1, N - P, P)

import concourse.mybir as mybir
from concourse.masks import make_identity

F32 = mybir.dt.float32
BF16 = mybir.dt.bfloat16
U16 = mybir.dt.uint16
COPY = mybir.ActivationFunctionType.Copy
SIGMOID = mybir.ActivationFunctionType.Sigmoid
ADD = mybir.AluOpType.add
MULT = mybir.AluOpType.mult

P = 128
SAMPLES = 8
PAIRS = SAMPLES // 2
STORE = 3072
N = 1536
HALF = 64
VALUE = 0
GATE = 1
BLOCKS = N // P
CHUNK = 512
CHUNKS = N // CHUNK
PER_BANK = CHUNK // P
PIECE = PER_BANK * P
PIECES = N // PIECE
SHORT = 2 * P
SHORTS = N // SHORT
LEAD = BLOCKS // 2
LAG = 2

FLOPS = 2 * SAMPLES * P * P * N + 2 * SAMPLES * P * N * N + 2 * PAIRS * P * N * N


def tile_stsgcm_b_kernel(tc, x, adj_t, w0, b0, offs, out):
    nc = tc.nc
    with (
        tc.tile_pool(name="held", bufs=1) as held,
        tc.tile_pool(name="work", bufs=2) as work,
        tc.tile_pool(name="pair", bufs=2 * (SHORTS + 1)) as pair,
        tc.tile_pool(name="swap", bufs=CHUNKS) as swap,
        tc.tile_pool(name="rounded", bufs=(LAG + 1) * CHUNKS) as rounded,
        tc.tile_pool(name="stored", bufs=2) as stored,
        tc.psum_pool(name="psum_small", bufs=2) as psum_small,
        tc.psum_pool(name="psum_sum", bufs=2 * CHUNKS) as psum_sum,
    ):
        offsets = held.tile([P, N // 16], U16, name="offsets")
        nc.sync.dma_start(offsets[:], offs)

        windows = [held.tile([P, STORE], F32, name=f"window{r}") for r in range(SAMPLES)]
        adj = [held.tile([P, N], BF16, name=f"adj{b}") for b in range(BLOCKS)]

        def load_window(r):
            nc.sync.dma_start(windows[r][:], x[r * P : (r + 1) * P, :])

        load_window(0)
        for b in range(BLOCKS):
            nc.sync.dma_start(adj[b][:], adj_t[b * P : (b + 1) * P, :])
            if b in (3, 5, 7):
                load_window((b - 1) // 2)
        bias = [held.tile([P, 1], F32, name=f"bias{h}") for h in (VALUE, GATE)]
        for h in (VALUE, GATE):
            for s in range(2):
                nc.sync.dma_start(
                    bias[h][s * HALF : (s + 1) * HALF, :], b0[h * HALF : (h + 1) * HALF, :]
                )
        for r in range(4, SAMPLES):
            load_window(r)

        w0_sb = held.tile([P, P], BF16, name="w0_sb")
        nc.scalar.dma_start(w0_sb[:], w0)

        w0_swapped = held.tile([P, P], BF16, name="w0_swapped")
        nc.vector.tensor_copy(w0_swapped[:, :HALF], w0_sb[:, HALF:])
        nc.vector.tensor_copy(w0_swapped[:, HALF:], w0_sb[:, :HALF])

        identity = held.tile([P, P], BF16, name="identity")
        make_identity(nc, identity[:])

        scratch = held.tile([P, 1], F32, name="scratch")
        nc.vector.memset(scratch[:], 0.0)
        nc.scalar.activation(scratch[:], scratch[:], SIGMOID)

        def look_up(r, first, width):
            entries = offsets[:, first // 16 : (first + width) // 16]
            picked = work.tile([P, width], F32, name="picked")
            nc.scalar.activation(picked[:], windows[r][:].indirect(entries), COPY)
            picked_bf = pair.tile([P, width], BF16, name="picked_bf")
            nc.vector.tensor_copy(picked_bf[:], picked[:])
            return picked_bf

        def look_up_pair(t):
            return [
                (r, g * PIECE, look_up(r, g * PIECE, PIECE))
                for r in (2 * t, 2 * t + 1)
                for g in range(PIECES)
            ]

        def mix(r, first, picked_bf):
            t, s = divmod(r, 2)
            blocks = picked_bf.shape[1] // P
            mix_ps = psum_small.tile([P, blocks, P], F32, name="mix_ps", tag="small")
            for i in range(blocks):
                nc.tensor.matmul(
                    mix_ps[:, i, :],
                    lhsT=picked_bf[:, i * P : (i + 1) * P],
                    rhs=w0_swapped[:] if r == 1 else w0_sb[:],
                    start=True,
                    stop=True,
                )
            if t == 0:
                nc.vector.tensor_copy(alone[:, first // P : first // P + blocks, s, :], mix_ps[:])
            else:
                nc.vector.tensor_copy(
                    mixed[t][:, first // P : first // P + blocks, :, s * HALF : (s + 1) * HALF],
                    mix_ps[:].rearrange("p b (h o) -> p b h o", h=2),
                )

        def add_block(total, stationary, b, first):
            nc.tensor.matmul(
                total[:],
                lhsT=stationary,
                rhs=adj[b][:, first : first + total.shape[1]],
                start=(b == 0),
                stop=(b == BLOCKS - 1),
            )

        def sum_over_vertices(stationary, first, width, to_flip=None):
            total = psum_sum.tile([P, width], F32, name="total")
            if to_flip is not None:
                t, c, h1_bf = to_flip
                flip_ps = psum_small.tile([P, PER_BANK, P], BF16, name="flip_ps", tag="small")
            for b in range(BLOCKS):
                add_block(total, stationary[b], b, first)
                if to_flip is not None and b < PER_BANK:
                    nc.tensor.transpose(flip_ps[:, b, :], h1_bf[:, b * P : (b + 1) * P], identity[:])
            if to_flip is not None:
                nc.vector.tensor_copy(
                    h1_flipped[t][:, c * PER_BANK : (c + 1) * PER_BANK, :], flip_ps[:]
                )
            return total

        def gated_unit(t, c, gate_ps, value_ps):
            gate = work.tile([P, CHUNK], F32, name="gate")
            nc.scalar.activation(gate[:], gate_ps[:], SIGMOID, bias=bias[GATE][:])
            h1 = stored.tile([P, CHUNK], F32, name="h1")
            nc.vector.scalar_tensor_tensor(
                h1[:], in0=value_ps[:], scalar=bias[VALUE][:], in1=gate[:], op0=ADD, op1=MULT
            )
            nc.sync.dma_start(out[t * P : (t + 1) * P, c * CHUNK : (c + 1) * CHUNK], h1[:])
            h1_bf = rounded.tile([P, CHUNK], BF16, name="h1_bf")
            nc.vector.tensor_copy(h1_bf[:], h1[:])
            return h1_bf

        def aggregate(t, first, width, to_flip=None):
            a1_ps = sum_over_vertices(
                [h1_flipped[t][:, b, :] for b in range(BLOCKS)], first, width, to_flip
            )
            a1 = stored.tile([P, width], F32, name="a1")
            nc.vector.tensor_copy(a1[:], a1_ps[:])
            nc.sync.dma_start(out[(PAIRS + t) * P : (PAIRS + t + 1) * P, first : first + width], a1[:])

        mixed = [None] + [held.tile([P, BLOCKS, 2, P], BF16, name=f"mixed{t}") for t in range(1, PAIRS)]
        alone = held.tile([P, BLOCKS, 2, P], BF16, name="alone")
        h1_flipped = [held.tile([P, BLOCKS, P], BF16, name=f"h1_flipped{t}") for t in range(PAIRS)]


        units = (
            [(0, b) for b in range(LEAD)]
            + [(1, b) for b in range(LEAD)]
            + [(s, b) for b in range(LEAD, BLOCKS) for s in range(2)]
        )
        firsts = [0, P] + [k * SHORT for k in range(1, SHORTS)]
        widths = [P, P] + [SHORT] * (SHORTS - 1)
        shorts = {
            (s, first // P): (s, first, look_up(s, first, width))
            for s in range(2)
            for first, width in zip(firsts, widths)
        }

        def mix_short(n):
            if n < len(units) and units[n] in shorts:
                mix(*shorts[units[n]])

        both = [
            [psum_sum.tile([P, CHUNK], F32, name="total") for c in range(CHUNKS)] for s in range(2)
        ]
        first_of_next = len(units) - 4 * PIECES
        mix_short(0)
        mix_short(1)
        for n, (s, b) in enumerate(units):
            mix_short(n + 2)
            for c in range(CHUNKS):
                add_block(both[s][c], alone[:, b, s, :], b, c * CHUNK)
            if n == first_of_next - 4:
                pieces = look_up_pair(1)
            if n >= first_of_next and n % 2 == 1:
                mix(*pieces[(n - first_of_next) // 2])

        value_rows = [slice(s * HALF, (s + 1) * HALF) for s in range(2)]
        gate_rows = [slice((1 - s) * HALF, (2 - s) * HALF) for s in range(2)]
        bias_alone = [held.tile([P, 1], F32, name=f"bias_alone{s}") for s in range(2)]
        for s in range(2):
            nc.vector.tensor_copy(bias_alone[s][value_rows[s], :], bias[VALUE][value_rows[s], :])
            nc.vector.tensor_copy(bias_alone[s][gate_rows[s], :], bias[GATE][gate_rows[s], :])
        lr = [[swap.tile([P, CHUNK], F32, name=f"lr{s}") for c in range(CHUNKS)] for s in range(2)]
        for s in range(2):
            for c in range(CHUNKS):
                nc.vector.tensor_scalar_add(lr[s][c][:], both[s][c][:], bias_alone[s][:])

        pieces = look_up_pair(2)

        h1_bf = {0: []}
        for c in range(CHUNKS):
            moved = swap.tile([P, CHUNK], F32, name="moved")
            h1 = swap.tile([P, CHUNK], F32, name="h1_late")
            for s in range(2):
                nc.scalar.activation(lr[s][c][gate_rows[s], :], lr[s][c][gate_rows[s], :], SIGMOID)
                nc.sync.dma_start(moved[value_rows[s], :], lr[s][c][gate_rows[s], :])
                nc.gpsimd.tensor_tensor(
                    h1[value_rows[s], :], lr[s][c][value_rows[s], :], moved[value_rows[s], :], MULT
                )
            nc.sync.dma_start(out[:P, c * CHUNK : (c + 1) * CHUNK], h1[:])
            rounded_h1 = rounded.tile([P, CHUNK], BF16, name="h1_bf")
            nc.gpsimd.tensor_copy(rounded_h1[:], h1[:])
            h1_bf[0].append(rounded_h1)

        def aggregate_pair(u):
            late = PAIRS - LAG <= u + 1 < PAIRS
            for c in range(CHUNKS if u + 1 < PAIRS else CHUNKS - 1):
                aggregate(u, c * CHUNK, CHUNK, to_flip=(u + 1, c, h1_bf[u + 1][c]) if late else None)

        for t in range(1, PAIRS):
            more = t + 1 < PAIRS
            h1_bf[t] = []
            for c in range(CHUNKS):
                gate_ps = sum_over_vertices(
                    [mixed[t][:, b, GATE, :] for b in range(BLOCKS)], c * CHUNK, CHUNK
                )
                if more:
                    mix(*pieces[2 * c])
                value_ps = sum_over_vertices(
                    [mixed[t][:, b, VALUE, :] for b in range(BLOCKS)],
                    c * CHUNK,
                    CHUNK,
                    to_flip=(t - LAG, c, h1_bf[t - LAG][c]) if t >= LAG else None,
                )
                if more:
                    mix(*pieces[2 * c + 1])
                h1_bf[t].append(gated_unit(t, c, gate_ps, value_ps))
            if t + 2 < PAIRS:
                pieces = look_up_pair(t + 2)
            if t >= LAG:
                aggregate_pair(t - LAG)
        for u in range(PAIRS - LAG, PAIRS):
            aggregate_pair(u)
        aggregate(PAIRS - 1, N - CHUNK, CHUNK - P)
        aggregate(PAIRS - 1, N - P, P)
